import numpy as np
import ml_dtypes


def mxq(x, axis, fmt="e4m3"):
    dtype, down = {"e4m3": (ml_dtypes.float8_e4m3fn, 7), "e5m2": (ml_dtypes.float8_e5m2, 14)}[fmt]
    v = np.moveaxis(np.asarray(x, np.float32).astype(ml_dtypes.bfloat16).astype(np.float64), axis, -1)
    blocks = v.reshape(v.shape[:-1] + (-1, 32))
    amax = np.abs(blocks).max(-1, keepdims=True)
    byte = np.maximum(np.where(amax > 0, np.frexp(amax)[1] - 1 + 127, 0) - down, 1)
    scale = np.exp2(byte - 127.0)
    codes = (blocks / scale).astype(np.float32).astype(dtype).astype(np.float64)
    return np.moveaxis((codes * scale).reshape(v.shape), -1, axis)


WIDE = False


def mx_kscale(k):
    if not WIDE:
        return np.ones(k)
    levels = np.array([10, -10, 5, -5, 0])
    a = np.random.permutation(np.resize(levels, k // 512 * 4)).reshape(k // 512, 4)
    idx = np.arange(k)
    return np.exp2(a[idx // 512, idx % 128 // 32])


BF16 = ml_dtypes.bfloat16


def bf(x):
    return np.asarray(x, np.float32).astype(BF16)


def f64(x):
    return np.asarray(x).astype(np.float64)


E2M1 = np.array([0.0, 0.5, 1.0, 1.5, 2.0, 3.0, 4.0, 6.0, -0.0, -0.5, -1.0, -1.5, -2.0, -3.0, -4.0, -6.0])


def pack_weight(w, fmt):
    k, n = w.shape
    w = f64(bf(w)).reshape(k // 32, 32, n)
    amax = np.abs(w).max(1)
    if fmt == "e4m3":
        byte = np.frexp(amax)[1] - 1 + 127 - 7
    else:
        mant, ex = np.frexp(amax / 6.0)
        byte = np.where(mant > 0.5, ex, ex - 1) + 127
    byte = np.clip(np.where(amax > 0, byte, 1), 1, 254)
    scaled = (w * np.exp2(127.0 - byte)[:, None, :]).reshape(k, n).astype(np.float32)
    by_word = np.ascontiguousarray(scaled.reshape(k // 512, 128, 4, n).transpose(0, 1, 3, 2))
    if fmt == "e4m3":
        words = by_word.astype(ml_dtypes.float8_e4m3fn).view(np.uint8)
    else:
        c = by_word.astype(ml_dtypes.float4_e2m1fn).view(np.uint8) & 0xF
        words = c[..., 0::2] | (c[..., 1::2] << 4)
    return np.ascontiguousarray(words), np.ascontiguousarray(byte.astype(np.uint8).reshape(k // 512, 16, n))


def unpack_weight(words, scales, fmt):
    g, p, n, _ = words.shape
    if fmt == "e4m3":
        vals = np.ascontiguousarray(words).view(ml_dtypes.float8_e4m3fn).astype(np.float64)
    else:
        nib = np.empty((g, p, n, 4), np.uint8)
        nib[..., 0::2] = words & 0xF
        nib[..., 1::2] = words >> 4
        vals = E2M1[nib]
    vals = vals * np.repeat(np.exp2(scales.astype(np.float64) - 127.0), 8, axis=1)[..., None]
    return vals.transpose(0, 1, 3, 2).reshape(g * 512, n)

def pack4(w):
    words, scales = pack_weight(w, "e2m1")
    return words.reshape(words.shape[0], 128, -1), scales


def unpack4(words, scales):
    return unpack_weight(words.reshape(words.shape[0], 128, -1, 2), scales, "e2m1")


B, IN_F, OUT_F, N_ACT = 2048, 1024, 1024, 4


def sigmoid(v):
    return 1.0 / (1.0 + np.exp(-v))


def setup_inputs():
    s = mx_kscale(IN_F)
    limit = np.sqrt(6.0 / (IN_F + OUT_F))
    x = bf(np.random.standard_normal((B, IN_F)) * s)
    w = np.random.uniform(-limit, limit, (OUT_F, IN_F)) / s[None, :]
    words, scales = pack4(np.ascontiguousarray(w.T))
    b = bf(np.random.standard_normal(OUT_F) * 0.1)
    return {"input": x,
            "W_words": words,
            "W_scales": scales,
            "b": b}


def _apply_cyclic_acts(y):
    Bb, O = y.shape
    yg = y.reshape(Bb, O // N_ACT, N_ACT)
    out = np.stack([
        np.tanh(yg[..., 0]),
        np.sin(yg[..., 1]),
        np.maximum(yg[..., 2], 0.0),
        sigmoid(yg[..., 3]),
    ], axis=-1)
    return out.reshape(Bb, O)


def reference(input, W_words, W_scales, b):
    y = (mxq(f64(input), 1, "e4m3") @ unpack4(W_words, W_scales)) + f64(b)
    return _apply_cyclic_acts(y)

@@ -1,0 +1,224 @@
+import math
+from contextlib import ExitStack
+
+import concourse.mybir as mybir
+from concourse.masks import make_identity
+
+F32 = mybir.dt.float32
+BF16 = mybir.dt.bfloat16
+I32 = mybir.dt.int32
+U32 = mybir.dt.uint32
+U8 = mybir.dt.uint8
+FP8X4 = mybir.dt.float8_e4m3fn_x4
+FP4X4 = mybir.dt.float4_e2m1fn_x4
+ACT = mybir.ActivationFunctionType
+ALU = mybir.AluOpType
+
+P = 128
+B, K, N = 2048, 1024, 1024
+FLOPS = 2 * B * K * N
+ROW_TILES = B // P
+GROUPS = K // 512
+HALVES = N // 512
+CLASSES = 4
+J_ALL = N // CLASSES
+J_BANK = 512 // CLASSES
+
+MANUAL = False
+UNITS = [(0, 1), (1, 1), (2, 2), (4, 2), (6, 2), (8, 2), (10, 2), (12, 2), (14, 1), (15, 1)]
+X_CHUNKS = [(0, 1), (1, 2), (2, 4), (4, 8), (8, 12), (12, 16)]
+V_SHARE = 0.375
+
+INV_2PI = 1.0 / (2.0 * math.pi)
+TWO_PI = 2.0 * math.pi
+
+
+def tile_vdl_kernel(tc, x, w_words, w_scales, b, out):
+    nc = tc.nc
+    x_v = x.rearrange("(p r) k -> p r k", r=ROW_TILES)
+    out_v = out.rearrange("(p r) n -> p r n", r=ROW_TILES)
+    n_units = len(UNITS)
+
+    with ExitStack() as ctx:
+        keep = ctx.enter_context(tc.tile_pool(name="keep", bufs=1))
+        stage = ctx.enter_context(tc.tile_pool(name="stage", bufs=3))
+        zpool = ctx.enter_context(tc.tile_pool(name="zpool", bufs=4))
+        opool = ctx.enter_context(tc.tile_pool(name="opool", bufs=3))
+        psum = ctx.enter_context(tc.psum_pool(name="psum", bufs=2))
+        if MANUAL:
+            ctx.enter_context(tc.manual_schedule())
+
+        x_sb = keep.tile([P, ROW_TILES, K], BF16, name="x_sb")
+        w_sb = keep.tile([P, GROUPS, 2 * N], U8, name="w_sb", align_bytes=64)
+        w_pl = keep.tile([P, GROUPS, N], U8, name="w_pl", align_bytes=64)
+        b_row = keep.tile([P, N], BF16, name="b_row")
+        ones = keep.tile([P, P], BF16, name="ones")
+        ident = keep.tile([P, P], F32, name="ident")
+        bias_pl = keep.tile([P, CLASSES, J_ALL], F32, name="bias_pl")
+        warm_in = keep.tile([P, 1], F32, name="warm_in")
+        warm_out = keep.tile([P, 1], F32, name="warm_out")
+
+        nc.vector.memset(warm_in[:], 0.0)
+        nc.vector.memset(w_pl[:].rearrange("p g n -> p (g n)").bitcast(I32), 0)
+        nc.vector.memset(b_row[:].bitcast(I32), 0)
+        nc.vector.memset(ones[:], 1.0)
+        make_identity(nc, ident[:])
+        nc.scalar.activation(out=warm_out[:], in_=warm_in[:], func=ACT.Silu)
+
+        def load_x(c):
+            r0, r1 = X_CHUNKS[c]
+            nc.sync.dma_start(out=x_sb[:, r0:r1, :], in_=x_v[:, r0:r1, :])
+
+        load_x(0)
+        nc.sync.dma_start(
+            out=w_sb[:].bitcast(I32),
+            in_=w_words.bitcast(I32).rearrange("g p n -> p g n"),
+        )
+        for r in range(4):
+            nc.sync.dma_start(
+                out=w_pl[r:P:32, :, :].bitcast(I32),
+                in_=w_scales[:, r:16:4, :].bitcast(I32).rearrange("g q n -> q g n"),
+            )
+        nc.sync.dma_start(out=b_row[0:1, :], in_=b.rearrange("(o n) -> o n", o=1))
+        for c in range(1, len(X_CHUNKS)):
+            load_x(c)
+
+        grouped, codes, xscl, ybank, zt, ot = {}, {}, {}, {}, {}, {}
+
+        def transposes(u):
+            r0, cnt = UNITS[u]
+            grouped[u] = stage.tile([P, cnt * K], BF16, name="grouped%d" % u, tag="grouped", align_bytes=64)
+            for i in range(cnt):
+                xw = x_sb[:, r0 + i, :].bitcast(F32)
+                xt = psum.tile([P, 512], F32, name="xt%d_%d" % (u, i), tag="xt", bufs=2)
+                for g in range(GROUPS):
+                    for h in range(2):
+                        q = 2 * g + h
+                        nc.tensor.transpose(
+                            xt[:, q * P : (q + 1) * P],
+                            xw[:, 256 * g + h : 256 * (g + 1) : 2],
+                            ident[:],
+                        )
+                nc.scalar.copy(
+                    out=grouped[u][:, i * K : (i + 1) * K].bitcast(F32).rearrange("p (g m h) -> p g m h", g=GROUPS, h=2),
+                    in_=xt[:].rearrange("p (g h m) -> p g m h", g=GROUPS, h=2),
+                )
+
+        def quantise(u):
+            r0, cnt = UNITS[u]
+            codes[u] = stage.tile([P, cnt * 256], U32, name="codes%d" % u, tag="codes", align_bytes=64)
+            xscl[u] = stage.tile([P, cnt * 256], U8, name="xscl%d" % u, tag="xscl", align_bytes=64)
+            nc.vector.quantize_mx(out=codes[u][:].bitcast(FP8X4), scales=xscl[u][:], in_=grouped[u][:])
+
+        def multiply(u):
+            r0, cnt = UNITS[u]
+            ybank[u] = []
+            for i in range(cnt):
+                for h in range(HALVES):
+                    y = psum.tile([P, 512], F32, name="y%d_%d_%d" % (u, i, h), tag="y", bufs=6)
+                    for g in range(GROUPS):
+                        c0 = i * 256 + g * P
+                        nc.tensor.matmul_mx(
+                            out=y[:],
+                            lhsT=codes[u][:, c0 : c0 + P].bitcast(FP8X4),
+                            lhsT_scale=xscl[u][:, c0 : c0 + P],
+                            rhs=w_sb[:, g, 1024 * h : 1024 * (h + 1)].bitcast(FP4X4),
+                            rhs_scale=w_pl[:, g, 512 * h : 512 * (h + 1)],
+                            start=(g == 0),
+                            stop=(g == GROUPS - 1),
+                        )
+                    ybank[u].append(y)
+
+        def add_bias(u, lo, hi):
+            r0, cnt = UNITS[u]
+            if lo == 0:
+                zt[u] = zpool.tile([P, CLASSES, cnt * J_ALL], F32, name="z%d" % u, tag="z")
+            for t in range(lo, hi):
+                i, h = divmod(t, HALVES)
+                c0 = i * J_ALL + h * J_BANK
+                nc.vector.tensor_tensor(
+                    out=zt[u][:, :, c0 : c0 + J_BANK],
+                    in0=ybank[u][t][:].rearrange("p (j a) -> p a j", a=CLASSES),
+                    in1=bias_pl[:, :, h * J_BANK : (h + 1) * J_BANK],
+                    op=ALU.add,
+                )
+
+        def vector_classes(u):
+            r0, cnt = UNITS[u]
+            z = zt[u]
+            turns = stage.tile([P, cnt * J_ALL], I32, name="turns%d" % u, tag="turns")
+            nc.vector.tensor_scalar(out=turns[:], in0=z[:, 1, :], scalar1=INV_2PI, scalar2=None, op0=ALU.mult)
+            nc.vector.scalar_tensor_tensor(
+                out=z[:, 1, :], in0=z[:, 1, :], scalar=INV_2PI, in1=turns[:], op0=ALU.mult, op1=ALU.subtract
+            )
+            nc.vector.tensor_scalar_max(z[:, 2, :], z[:, 2, :], 0.0)
+
+        def scalar_classes(u):
+            z = zt[u]
+            nc.scalar.activation(out=z[:, 3, :], in_=z[:, 3, :], func=ACT.Tanh, scale=0.5)
+            nc.scalar.activation(out=z[:, 0, :], in_=z[:, 0, :], func=ACT.Tanh)
+            nc.scalar.activation(out=z[:, 1, :], in_=z[:, 1, :], func=ACT.Sin, scale=TWO_PI)
+
+        def sigmoid_affine(u):
+            z = zt[u]
+            nc.vector.tensor_scalar(
+                out=z[:, 3, :], in0=z[:, 3, :], scalar1=0.5, scalar2=0.5, op0=ALU.mult, op1=ALU.add
+            )
+
+        def split_point(u):
+            r0, cnt = UNITS[u]
+            return 8 * int(round(V_SHARE * cnt * J_ALL / 8.0))
+
+        def views(u, lo, hi):
+            o_view = ot[u][:, CLASSES * lo : CLASSES * hi].rearrange("p (l a) -> p l a", a=CLASSES)
+            z_view = zt[u][:, :, lo:hi].rearrange("p a l -> p l a")
+            return o_view, z_view
+
+        def interleave_scalar(u):
+            r0, cnt = UNITS[u]
+            ot[u] = opool.tile([P, cnt * N], F32, name="o%d" % u, tag="o")
+            o_view, z_view = views(u, split_point(u), cnt * J_ALL)
+            nc.scalar.copy(out=o_view, in_=z_view)
+
+        def interleave_vector(u):
+            o_view, z_view = views(u, 0, split_point(u))
+            nc.vector.tensor_copy(out=o_view, in_=z_view)
+
+        def store(u):
+            r0, cnt = UNITS[u]
+            nc.sync.dma_start(out=out_v[:, r0 : r0 + cnt, :], in_=ot[u][:].rearrange("p (r n) -> p r n", r=cnt))
+
+        transposes(0)
+        transposes(1)
+        for h in range(HALVES):
+            pb = psum.tile([P, 512], F32, name="pb%d" % h, tag="y", bufs=6)
+            nc.tensor.matmul(out=pb[:], lhsT=ones[:], rhs=b_row[:, 512 * h : 512 * (h + 1)], start=True, stop=True)
+            nc.vector.tensor_copy(
+                out=bias_pl[:, :, h * J_BANK : (h + 1) * J_BANK],
+                in_=pb[:].rearrange("p (j a) -> p a j", a=CLASSES),
+            )
+        quantise(0)
+        multiply(0)
+        transposes(2)
+        quantise(1)
+
+        for s in range(n_units + 1):
+            if s + 3 < n_units:
+                transposes(s + 3)
+            if s + 1 < n_units:
+                multiply(s + 1)
+            if s < n_units:
+                banks = len(ybank[s])
+                add_bias(s, 0, banks // 2)
+            if s >= 1:
+                sigmoid_affine(s - 1)
+                interleave_scalar(s - 1)
+            if s < n_units:
+                add_bias(s, banks // 2, banks)
+                vector_classes(s)
+                scalar_classes(s)
+            if s + 2 < n_units:
+                quantise(s + 2)
+            if s >= 1:
+                interleave_vector(s - 1)
+                store(s - 1)

@@ -27,10 +27,13 @@ J_BANK = 512 // CLASSES
 MANUAL = False
 UNITS = [(0, 1), (1, 1), (2, 2), (4, 2), (6, 2), (8, 2), (10, 2), (12, 2), (14, 1), (15, 1)]
 X_CHUNKS = [(0, 1), (1, 2), (2, 4), (4, 8), (8, 12), (12, 16)]
-V_SHARE = 0.375
+POOL_UNTIL = 8
+V_SHARE_POOL = 0.42
+V_SHARE_LAST = 0.625
 
 INV_2PI = 1.0 / (2.0 * math.pi)
 TWO_PI = 2.0 * math.pi
+BIG = 3.0e38
 
 
 def tile_vdl_kernel(tc, x, w_words, w_scales, b, out):
@@ -42,8 +45,8 @@ def tile_vdl_kernel(tc, x, w_words, w_scales, b, out):
     with ExitStack() as ctx:
         keep = ctx.enter_context(tc.tile_pool(name="keep", bufs=1))
         stage = ctx.enter_context(tc.tile_pool(name="stage", bufs=3))
-        zpool = ctx.enter_context(tc.tile_pool(name="zpool", bufs=4))
-        opool = ctx.enter_context(tc.tile_pool(name="opool", bufs=3))
+        zpool = ctx.enter_context(tc.tile_pool(name="zpool", bufs=5))
+        opool = ctx.enter_context(tc.tile_pool(name="opool", bufs=4))
         psum = ctx.enter_context(tc.psum_pool(name="psum", bufs=2))
         if MANUAL:
             ctx.enter_context(tc.manual_schedule())
@@ -83,11 +86,13 @@ def tile_vdl_kernel(tc, x, w_words, w_scales, b, out):
         for c in range(1, len(X_CHUNKS)):
             load_x(c)
 
-        grouped, codes, xscl, ybank, zt, ot = {}, {}, {}, {}, {}, {}
+        xts, grouped, codes, xscl, ybank, zt, ot = {}, {}, {}, {}, {}, {}, {}
 
         def transposes(u):
+            if u >= n_units:
+                return
             r0, cnt = UNITS[u]
-            grouped[u] = stage.tile([P, cnt * K], BF16, name="grouped%d" % u, tag="grouped", align_bytes=64)
+            xts[u] = []
             for i in range(cnt):
                 xw = x_sb[:, r0 + i, :].bitcast(F32)
                 xt = psum.tile([P, 512], F32, name="xt%d_%d" % (u, i), tag="xt", bufs=2)
@@ -99,18 +104,30 @@ def tile_vdl_kernel(tc, x, w_words, w_scales, b, out):
                             xw[:, 256 * g + h : 256 * (g + 1) : 2],
                             ident[:],
                         )
+                xts[u].append(xt)
+
+        def copy_out(u):
+            if u >= n_units:
+                return
+            r0, cnt = UNITS[u]
+            grouped[u] = stage.tile([P, cnt * K], BF16, name="grouped%d" % u, tag="grouped", align_bytes=64)
+            for i in range(cnt):
                 nc.scalar.copy(
                     out=grouped[u][:, i * K : (i + 1) * K].bitcast(F32).rearrange("p (g m h) -> p g m h", g=GROUPS, h=2),
-                    in_=xt[:].rearrange("p (g h m) -> p g m h", g=GROUPS, h=2),
+                    in_=xts[u][i][:].rearrange("p (g h m) -> p g m h", g=GROUPS, h=2),
                 )
 
         def quantise(u):
+            if u >= n_units:
+                return
             r0, cnt = UNITS[u]
             codes[u] = stage.tile([P, cnt * 256], U32, name="codes%d" % u, tag="codes", align_bytes=64)
             xscl[u] = stage.tile([P, cnt * 256], U8, name="xscl%d" % u, tag="xscl", align_bytes=64)
             nc.vector.quantize_mx(out=codes[u][:].bitcast(FP8X4), scales=xscl[u][:], in_=grouped[u][:])
 
         def multiply(u):
+            if u >= n_units:
+                return
             r0, cnt = UNITS[u]
             ybank[u] = []
             for i in range(cnt):
@@ -129,11 +146,10 @@ def tile_vdl_kernel(tc, x, w_words, w_scales, b, out):
                         )
                     ybank[u].append(y)
 
-        def add_bias(u, lo, hi):
+        def add_bias(u):
             r0, cnt = UNITS[u]
-            if lo == 0:
-                zt[u] = zpool.tile([P, CLASSES, cnt * J_ALL], F32, name="z%d" % u, tag="z")
-            for t in range(lo, hi):
+            zt[u] = zpool.tile([P, CLASSES, cnt * J_ALL], F32, name="z%d" % u, tag="z")
+            for t in range(cnt * HALVES):
                 i, h = divmod(t, HALVES)
                 c0 = i * J_ALL + h * J_BANK
                 nc.vector.tensor_tensor(
@@ -143,7 +159,7 @@ def tile_vdl_kernel(tc, x, w_words, w_scales, b, out):
                     op=ALU.add,
                 )
 
-        def vector_classes(u):
+        def reduce_angle(u):
             r0, cnt = UNITS[u]
             z = zt[u]
             turns = stage.tile([P, cnt * J_ALL], I32, name="turns%d" % u, tag="turns")
@@ -151,7 +167,11 @@ def tile_vdl_kernel(tc, x, w_words, w_scales, b, out):
             nc.vector.scalar_tensor_tensor(
                 out=z[:, 1, :], in0=z[:, 1, :], scalar=INV_2PI, in1=turns[:], op0=ALU.mult, op1=ALU.subtract
             )
-            nc.vector.tensor_scalar_max(z[:, 2, :], z[:, 2, :], 0.0)
+
+        def relu_and_affine(u, eng):
+            z = zt[u]
+            eng.tensor_scalar(out=z[:, 2, :], in0=z[:, 2, :], scalar1=BIG, scalar2=0.0, op0=ALU.min, op1=ALU.max)
+            eng.tensor_scalar(out=z[:, 3, :], in0=z[:, 3, :], scalar1=0.5, scalar2=0.5, op0=ALU.mult, op1=ALU.add)
 
         def scalar_classes(u):
             z = zt[u]
@@ -159,15 +179,10 @@ def tile_vdl_kernel(tc, x, w_words, w_scales, b, out):
             nc.scalar.activation(out=z[:, 0, :], in_=z[:, 0, :], func=ACT.Tanh)
             nc.scalar.activation(out=z[:, 1, :], in_=z[:, 1, :], func=ACT.Sin, scale=TWO_PI)
 
-        def sigmoid_affine(u):
-            z = zt[u]
-            nc.vector.tensor_scalar(
-                out=z[:, 3, :], in0=z[:, 3, :], scalar1=0.5, scalar2=0.5, op0=ALU.mult, op1=ALU.add
-            )
-
         def split_point(u):
             r0, cnt = UNITS[u]
-            return 8 * int(round(V_SHARE * cnt * J_ALL / 8.0))
+            share = V_SHARE_POOL if u < POOL_UNTIL else V_SHARE_LAST
+            return 8 * int(round(share * cnt * J_ALL / 8.0))
 
         def views(u, lo, hi):
             o_view = ot[u][:, CLASSES * lo : CLASSES * hi].rearrange("p (l a) -> p l a", a=CLASSES)
@@ -189,7 +204,9 @@ def tile_vdl_kernel(tc, x, w_words, w_scales, b, out):
             nc.sync.dma_start(out=out_v[:, r0 : r0 + cnt, :], in_=ot[u][:].rearrange("p (r n) -> p r n", r=cnt))
 
         transposes(0)
+        copy_out(0)
         transposes(1)
+        copy_out(1)
         for h in range(HALVES):
             pb = psum.tile([P, 512], F32, name="pb%d" % h, tag="y", bufs=6)
             nc.tensor.matmul(out=pb[:], lhsT=ones[:], rhs=b_row[:, 512 * h : 512 * (h + 1)], start=True, stop=True)
@@ -200,25 +217,30 @@ def tile_vdl_kernel(tc, x, w_words, w_scales, b, out):
         quantise(0)
         multiply(0)
         transposes(2)
+        copy_out(2)
         quantise(1)
 
         for s in range(n_units + 1):
-            if s + 3 < n_units:
-                transposes(s + 3)
-            if s + 1 < n_units:
-                multiply(s + 1)
+            late = s - 1 if (s >= 1 and s - 1 < POOL_UNTIL) else None
+            multiply(s + 1)
+            transposes(s + 3)
             if s < n_units:
-                banks = len(ybank[s])
-                add_bias(s, 0, banks // 2)
-            if s >= 1:
-                sigmoid_affine(s - 1)
-                interleave_scalar(s - 1)
+                add_bias(s)
+            if late is not None:
+                relu_and_affine(late, nc.gpsimd)
             if s < n_units:
-                add_bias(s, banks // 2, banks)
-                vector_classes(s)
+                reduce_angle(s)
+            if late is not None:
+                interleave_scalar(late)
+            if s < n_units:
                 scalar_classes(s)
-            if s + 2 < n_units:
-                quantise(s + 2)
-            if s >= 1:
-                interleave_vector(s - 1)
-                store(s - 1)
+            copy_out(s + 3)
+            quantise(s + 2)
+            if late is not None:
+                interleave_vector(late)
+                store(late)
+            if s < n_units and s >= POOL_UNTIL:
+                relu_and_affine(s, nc.vector)
+                interleave_scalar(s)
+                interleave_vector(s)
+                store(s)

@@ -25,9 +25,9 @@ J_ALL = N // CLASSES
 J_BANK = 512 // CLASSES
 
 MANUAL = False
-UNITS = [(0, 1), (1, 1), (2, 2), (4, 2), (6, 2), (8, 2), (10, 2), (12, 2), (14, 1), (15, 1)]
+UNITS = [(0, 1), (1, 1), (2, 1), (3, 1), (4, 1), (5, 1), (6, 1), (7, 1), (8, 1), (9, 1), (10, 1), (11, 1), (12, 1), (13, 1), (14, 1), (15, 1)]
 X_CHUNKS = [(0, 1), (1, 2), (2, 4), (4, 8), (8, 12), (12, 16)]
-POOL_UNTIL = 8
+POOL_UNTIL = 14
 V_SHARE_POOL = 0.42
 V_SHARE_LAST = 0.625
 
@@ -44,9 +44,9 @@ def tile_vdl_kernel(tc, x, w_words, w_scales, b, out):
 
     with ExitStack() as ctx:
         keep = ctx.enter_context(tc.tile_pool(name="keep", bufs=1))
-        stage = ctx.enter_context(tc.tile_pool(name="stage", bufs=3))
-        zpool = ctx.enter_context(tc.tile_pool(name="zpool", bufs=5))
-        opool = ctx.enter_context(tc.tile_pool(name="opool", bufs=4))
+        stage = ctx.enter_context(tc.tile_pool(name="stage", bufs=5))
+        zpool = ctx.enter_context(tc.tile_pool(name="zpool", bufs=8))
+        opool = ctx.enter_context(tc.tile_pool(name="opool", bufs=6))
         psum = ctx.enter_context(tc.psum_pool(name="psum", bufs=2))
         if MANUAL:
             ctx.enter_context(tc.manual_schedule())
@@ -72,7 +72,9 @@ def tile_vdl_kernel(tc, x, w_words, w_scales, b, out):
             r0, r1 = X_CHUNKS[c]
             nc.sync.dma_start(out=x_sb[:, r0:r1, :], in_=x_v[:, r0:r1, :])
 
+        nc.sync.dma_start(out=b_row[0:1, :], in_=b.rearrange("(o n) -> o n", o=1))
         load_x(0)
+        load_x(1)
         nc.sync.dma_start(
             out=w_sb[:].bitcast(I32),
             in_=w_words.bitcast(I32).rearrange("g p n -> p g n"),
@@ -82,8 +84,7 @@ def tile_vdl_kernel(tc, x, w_words, w_scales, b, out):
                 out=w_pl[r:P:32, :, :].bitcast(I32),
                 in_=w_scales[:, r:16:4, :].bitcast(I32).rearrange("g q n -> q g n"),
             )
-        nc.sync.dma_start(out=b_row[0:1, :], in_=b.rearrange("(o n) -> o n", o=1))
-        for c in range(1, len(X_CHUNKS)):
+        for c in range(2, len(X_CHUNKS)):
             load_x(c)
 
         xts, grouped, codes, xscl, ybank, zt, ot = {}, {}, {}, {}, {}, {}, {}

@@ -30,6 +30,7 @@ X_CHUNKS = [(0, 1), (1, 2), (2, 4), (4, 8), (8, 12), (12, 16)]
 POOL_UNTIL = 14
 V_SHARE_POOL = 0.42
 V_SHARE_LAST = 0.625
+LAST_HALF_V = 80
 
 INV_2PI = 1.0 / (2.0 * math.pi)
 TWO_PI = 2.0 * math.pi
@@ -160,25 +161,37 @@ def tile_vdl_kernel(tc, x, w_words, w_scales, b, out):
                     op=ALU.add,
                 )
 
-        def reduce_angle(u):
-            r0, cnt = UNITS[u]
+        def reduce_angle(u, lo=0, hi=J_ALL):
             z = zt[u]
-            turns = stage.tile([P, cnt * J_ALL], I32, name="turns%d" % u, tag="turns")
-            nc.vector.tensor_scalar(out=turns[:], in0=z[:, 1, :], scalar1=INV_2PI, scalar2=None, op0=ALU.mult)
+            turns = stage.tile([P, hi - lo], I32, name="turns%d_%d" % (u, lo), tag="turns")
+            nc.vector.tensor_scalar(out=turns[:], in0=z[:, 1, lo:hi], scalar1=INV_2PI, scalar2=None, op0=ALU.mult)
             nc.vector.scalar_tensor_tensor(
-                out=z[:, 1, :], in0=z[:, 1, :], scalar=INV_2PI, in1=turns[:], op0=ALU.mult, op1=ALU.subtract
+                out=z[:, 1, lo:hi], in0=z[:, 1, lo:hi], scalar=INV_2PI, in1=turns[:], op0=ALU.mult, op1=ALU.subtract
             )
 
-        def relu_and_affine(u, eng):
+        def relu_and_affine(u, eng, lo=0, hi=J_ALL):
             z = zt[u]
-            eng.tensor_scalar(out=z[:, 2, :], in0=z[:, 2, :], scalar1=BIG, scalar2=0.0, op0=ALU.min, op1=ALU.max)
-            eng.tensor_scalar(out=z[:, 3, :], in0=z[:, 3, :], scalar1=0.5, scalar2=0.5, op0=ALU.mult, op1=ALU.add)
+            eng.tensor_scalar(out=z[:, 2, lo:hi], in0=z[:, 2, lo:hi], scalar1=BIG, scalar2=0.0, op0=ALU.min, op1=ALU.max)
+            eng.tensor_scalar(out=z[:, 3, lo:hi], in0=z[:, 3, lo:hi], scalar1=0.5, scalar2=0.5, op0=ALU.mult, op1=ALU.add)
 
-        def scalar_classes(u):
+        def scalar_classes(u, lo=0, hi=J_ALL):
             z = zt[u]
-            nc.scalar.activation(out=z[:, 3, :], in_=z[:, 3, :], func=ACT.Tanh, scale=0.5)
-            nc.scalar.activation(out=z[:, 0, :], in_=z[:, 0, :], func=ACT.Tanh)
-            nc.scalar.activation(out=z[:, 1, :], in_=z[:, 1, :], func=ACT.Sin, scale=TWO_PI)
+            nc.scalar.activation(out=z[:, 3, lo:hi], in_=z[:, 3, lo:hi], func=ACT.Tanh, scale=0.5)
+            nc.scalar.activation(out=z[:, 0, lo:hi], in_=z[:, 0, lo:hi], func=ACT.Tanh)
+            nc.scalar.activation(out=z[:, 1, lo:hi], in_=z[:, 1, lo:hi], func=ACT.Sin, scale=TWO_PI)
+
+        def last_half(u, h):
+            r0, cnt = UNITS[u]
+            lo, hi = h * J_BANK, (h + 1) * J_BANK
+            cut = lo + LAST_HALF_V
+            reduce_angle(u, lo, hi)
+            scalar_classes(u, lo, hi)
+            relu_and_affine(u, nc.vector, lo, hi)
+            o_view, z_view = views(u, cut, hi)
+            nc.scalar.copy(out=o_view, in_=z_view)
+            o_view, z_view = views(u, lo, cut)
+            nc.vector.tensor_copy(out=o_view, in_=z_view)
+            nc.sync.dma_start(out=out_v[:, r0, CLASSES * lo : CLASSES * hi], in_=ot[u][:, CLASSES * lo : CLASSES * hi])
 
         def split_point(u):
             r0, cnt = UNITS[u]
@@ -229,18 +242,22 @@ def tile_vdl_kernel(tc, x, w_words, w_scales, b, out):
                 add_bias(s)
             if late is not None:
                 relu_and_affine(late, nc.gpsimd)
-            if s < n_units:
+            if s < n_units - 1:
                 reduce_angle(s)
             if late is not None:
                 interleave_scalar(late)
-            if s < n_units:
+            if s < n_units - 1:
                 scalar_classes(s)
+            if s == n_units - 1:
+                ot[s] = opool.tile([P, N], F32, name="o%d" % s, tag="o")
+                last_half(s, 0)
+                last_half(s, 1)
             copy_out(s + 3)
             quantise(s + 2)
             if late is not None:
                 interleave_vector(late)
                 store(late)
-            if s < n_units and s >= POOL_UNTIL:
+            if s == n_units - 2:
                 relu_and_affine(s, nc.vector)
                 interleave_scalar(s)
                 interleave_vector(s)

@@ -199,8 +199,8 @@ def tile_vdl_kernel(tc, x, w_words, w_scales, b, out):
             return 8 * int(round(share * cnt * J_ALL / 8.0))
 
         def views(u, lo, hi):
-            o_view = ot[u][:, CLASSES * lo : CLASSES * hi].rearrange("p (l a) -> p l a", a=CLASSES)
-            z_view = zt[u][:, :, lo:hi].rearrange("p a l -> p l a")
+            o_view = ot[u][:, CLASSES * lo : CLASSES * hi].rearrange("p (c i a) -> p c a i", i=4, a=CLASSES)
+            z_view = zt[u][:, :, lo:hi].rearrange("p a (c i) -> p c a i", i=4)
             return o_view, z_view
 
         def interleave_scalar(u):

import math
from contextlib import ExitStack

import concourse.mybir as mybir
from concourse.masks import make_identity

F32 = mybir.dt.float32
BF16 = mybir.dt.bfloat16
I32 = mybir.dt.int32
U32 = mybir.dt.uint32
U8 = mybir.dt.uint8
FP8X4 = mybir.dt.float8_e4m3fn_x4
FP4X4 = mybir.dt.float4_e2m1fn_x4
ACT = mybir.ActivationFunctionType
ALU = mybir.AluOpType

P = 128
B, K, N = 2048, 1024, 1024
FLOPS = 2 * B * K * N
ROW_TILES = B // P
GROUPS = K // 512
HALVES = N // 512
CLASSES = 4
J_ALL = N // CLASSES
J_BANK = 512 // CLASSES

MANUAL = False
UNITS = [(0, 1), (1, 1), (2, 1), (3, 1), (4, 1), (5, 1), (6, 1), (7, 1), (8, 1), (9, 1), (10, 1), (11, 1), (12, 1), (13, 1), (14, 1), (15, 1)]
X_CHUNKS = [(0, 1), (1, 2), (2, 4), (4, 8), (8, 12), (12, 16)]
POOL_UNTIL = 14
V_SHARE_POOL = 0.42
V_SHARE_LAST = 0.625
LAST_HALF_V = 80

INV_2PI = 1.0 / (2.0 * math.pi)
TWO_PI = 2.0 * math.pi
BIG = 3.0e38


def tile_vdl_kernel(tc, x, w_words, w_scales, b, out):
    nc = tc.nc
    x_v = x.rearrange("(p r) k -> p r k", r=ROW_TILES)
    out_v = out.rearrange("(p r) n -> p r n", r=ROW_TILES)
    n_units = len(UNITS)

    with ExitStack() as ctx:
        keep = ctx.enter_context(tc.tile_pool(name="keep", bufs=1))
        stage = ctx.enter_context(tc.tile_pool(name="stage", bufs=5))
        zpool = ctx.enter_context(tc.tile_pool(name="zpool", bufs=8))
        opool = ctx.enter_context(tc.tile_pool(name="opool", bufs=6))
        psum = ctx.enter_context(tc.psum_pool(name="psum", bufs=2))
        if MANUAL:
            ctx.enter_context(tc.manual_schedule())

        x_sb = keep.tile([P, ROW_TILES, K], BF16, name="x_sb")
        w_sb = keep.tile([P, GROUPS, 2 * N], U8, name="w_sb", align_bytes=64)
        w_pl = keep.tile([P, GROUPS, N], U8, name="w_pl", align_bytes=64)
        b_row = keep.tile([P, N], BF16, name="b_row")
        ones = keep.tile([P, P], BF16, name="ones")
        ident = keep.tile([P, P], F32, name="ident")
        bias_pl = keep.tile([P, CLASSES, J_ALL], F32, name="bias_pl")
        warm_in = keep.tile([P, 1], F32, name="warm_in")
        warm_out = keep.tile([P, 1], F32, name="warm_out")

        nc.vector.memset(warm_in[:], 0.0)
        nc.vector.memset(w_pl[:].rearrange("p g n -> p (g n)").bitcast(I32), 0)
        nc.vector.memset(b_row[:].bitcast(I32), 0)
        nc.vector.memset(ones[:], 1.0)
        make_identity(nc, ident[:])
        nc.scalar.activation(out=warm_out[:], in_=warm_in[:], func=ACT.Silu)

        def load_x(c):
            r0, r1 = X_CHUNKS[c]
            nc.sync.dma_start(out=x_sb[:, r0:r1, :], in_=x_v[:, r0:r1, :])

        nc.sync.dma_start(out=b_row[0:1, :], in_=b.rearrange("(o n) -> o n", o=1))
        load_x(0)
        load_x(1)
        nc.sync.dma_start(
            out=w_sb[:].bitcast(I32),
            in_=w_words.bitcast(I32).rearrange("g p n -> p g n"),
        )
        for r in range(4):
            nc.sync.dma_start(
                out=w_pl[r:P:32, :, :].bitcast(I32),
                in_=w_scales[:, r:16:4, :].bitcast(I32).rearrange("g q n -> q g n"),
            )
        for c in range(2, len(X_CHUNKS)):
            load_x(c)

        xts, grouped, codes, xscl, ybank, zt, ot = {}, {}, {}, {}, {}, {}, {}

        def transposes(u):
            if u >= n_units:
                return
            r0, cnt = UNITS[u]
            xts[u] = []
            for i in range(cnt):
                xw = x_sb[:, r0 + i, :].bitcast(F32)
                xt = psum.tile([P, 512], F32, name="xt%d_%d" % (u, i), tag="xt", bufs=2)
                for g in range(GROUPS):
                    for h in range(2):
                        q = 2 * g + h
                        nc.tensor.transpose(
                            xt[:, q * P : (q + 1) * P],
                            xw[:, 256 * g + h : 256 * (g + 1) : 2],
                            ident[:],
                        )
                xts[u].append(xt)

        def copy_out(u):
            if u >= n_units:
                return
            r0, cnt = UNITS[u]
            grouped[u] = stage.tile([P, cnt * K], BF16, name="grouped%d" % u, tag="grouped", align_bytes=64)
            for i in range(cnt):
                nc.scalar.copy(
                    out=grouped[u][:, i * K : (i + 1) * K].bitcast(F32).rearrange("p (g m h) -> p g m h", g=GROUPS, h=2),
                    in_=xts[u][i][:].rearrange("p (g h m) -> p g m h", g=GROUPS, h=2),
                )

        def quantise(u):
            if u >= n_units:
                return
            r0, cnt = UNITS[u]
            codes[u] = stage.tile([P, cnt * 256], U32, name="codes%d" % u, tag="codes", align_bytes=64)
            xscl[u] = stage.tile([P, cnt * 256], U8, name="xscl%d" % u, tag="xscl", align_bytes=64)
            nc.vector.quantize_mx(out=codes[u][:].bitcast(FP8X4), scales=xscl[u][:], in_=grouped[u][:])

        def multiply(u):
            if u >= n_units:
                return
            r0, cnt = UNITS[u]
            ybank[u] = []
            for i in range(cnt):
                for h in range(HALVES):
                    y = psum.tile([P, 512], F32, name="y%d_%d_%d" % (u, i, h), tag="y", bufs=6)
                    for g in range(GROUPS):
                        c0 = i * 256 + g * P
                        nc.tensor.matmul_mx(
                            out=y[:],
                            lhsT=codes[u][:, c0 : c0 + P].bitcast(FP8X4),
                            lhsT_scale=xscl[u][:, c0 : c0 + P],
                            rhs=w_sb[:, g, 1024 * h : 1024 * (h + 1)].bitcast(FP4X4),
                            rhs_scale=w_pl[:, g, 512 * h : 512 * (h + 1)],
                            start=(g == 0),
                            stop=(g == GROUPS - 1),
                        )
                    ybank[u].append(y)

        def add_bias(u):
            r0, cnt = UNITS[u]
            zt[u] = zpool.tile([P, CLASSES, cnt * J_ALL], F32, name="z%d" % u, tag="z")
            for t in range(cnt * HALVES):
                i, h = divmod(t, HALVES)
                c0 = i * J_ALL + h * J_BANK
                nc.vector.tensor_tensor(
                    out=zt[u][:, :, c0 : c0 + J_BANK],
                    in0=ybank[u][t][:].rearrange("p (j a) -> p a j", a=CLASSES),
                    in1=bias_pl[:, :, h * J_BANK : (h + 1) * J_BANK],
                    op=ALU.add,
                )

        def reduce_angle(u, lo=0, hi=J_ALL):
            z = zt[u]
            turns = stage.tile([P, hi - lo], I32, name="turns%d_%d" % (u, lo), tag="turns")
            nc.vector.tensor_scalar(out=turns[:], in0=z[:, 1, lo:hi], scalar1=INV_2PI, scalar2=None, op0=ALU.mult)
            nc.vector.scalar_tensor_tensor(
                out=z[:, 1, lo:hi], in0=z[:, 1, lo:hi], scalar=INV_2PI, in1=turns[:], op0=ALU.mult, op1=ALU.subtract
            )

        def relu_and_affine(u, eng, lo=0, hi=J_ALL):
            z = zt[u]
            eng.tensor_scalar(out=z[:, 2, lo:hi], in0=z[:, 2, lo:hi], scalar1=BIG, scalar2=0.0, op0=ALU.min, op1=ALU.max)
            eng.tensor_scalar(out=z[:, 3, lo:hi], in0=z[:, 3, lo:hi], scalar1=0.5, scalar2=0.5, op0=ALU.mult, op1=ALU.add)

        def scalar_classes(u, lo=0, hi=J_ALL):
            z = zt[u]
            nc.scalar.activation(out=z[:, 3, lo:hi], in_=z[:, 3, lo:hi], func=ACT.Tanh, scale=0.5)
            nc.scalar.activation(out=z[:, 0, lo:hi], in_=z[:, 0, lo:hi], func=ACT.Tanh)
            nc.scalar.activation(out=z[:, 1, lo:hi], in_=z[:, 1, lo:hi], func=ACT.Sin, scale=TWO_PI)

        def last_half(u, h):
            r0, cnt = UNITS[u]
            lo, hi = h * J_BANK, (h + 1) * J_BANK
            cut = lo + LAST_HALF_V
            reduce_angle(u, lo, hi)
            scalar_classes(u, lo, hi)
            relu_and_affine(u, nc.vector, lo, hi)
            o_view, z_view = views(u, cut, hi)
            nc.scalar.copy(out=o_view, in_=z_view)
            o_view, z_view = views(u, lo, cut)
            nc.vector.tensor_copy(out=o_view, in_=z_view)
            nc.sync.dma_start(out=out_v[:, r0, CLASSES * lo : CLASSES * hi], in_=ot[u][:, CLASSES * lo : CLASSES * hi])

        def split_point(u):
            r0, cnt = UNITS[u]
            share = V_SHARE_POOL if u < POOL_UNTIL else V_SHARE_LAST
            return 8 * int(round(share * cnt * J_ALL / 8.0))

        def views(u, lo, hi):
            o_view = ot[u][:, CLASSES * lo : CLASSES * hi].rearrange("p (c i a) -> p c a i", i=4, a=CLASSES)
            z_view = zt[u][:, :, lo:hi].rearrange("p a (c i) -> p c a i", i=4)
            return o_view, z_view

        def interleave_scalar(u):
            r0, cnt = UNITS[u]
            ot[u] = opool.tile([P, cnt * N], F32, name="o%d" % u, tag="o")
            o_view, z_view = views(u, split_point(u), cnt * J_ALL)
            nc.scalar.copy(out=o_view, in_=z_view)

        def interleave_vector(u):
            o_view, z_view = views(u, 0, split_point(u))
            nc.vector.tensor_copy(out=o_view, in_=z_view)

        def store(u):
            r0, cnt = UNITS[u]
            nc.sync.dma_start(out=out_v[:, r0 : r0 + cnt, :], in_=ot[u][:].rearrange("p (r n) -> p r n", r=cnt))

        transposes(0)
        copy_out(0)
        transposes(1)
        copy_out(1)
        for h in range(HALVES):
            pb = psum.tile([P, 512], F32, name="pb%d" % h, tag="y", bufs=6)
            nc.tensor.matmul(out=pb[:], lhsT=ones[:], rhs=b_row[:, 512 * h : 512 * (h + 1)], start=True, stop=True)
            nc.vector.tensor_copy(
                out=bias_pl[:, :, h * J_BANK : (h + 1) * J_BANK],
                in_=pb[:].rearrange("p (j a) -> p a j", a=CLASSES),
            )
        quantise(0)
        multiply(0)
        transposes(2)
        copy_out(2)
        quantise(1)

        for s in range(n_units + 1):
            late = s - 1 if (s >= 1 and s - 1 < POOL_UNTIL) else None
            multiply(s + 1)
            transposes(s + 3)
            if s < n_units:
                add_bias(s)
            if late is not None:
                relu_and_affine(late, nc.gpsimd)
            if s < n_units - 1:
                reduce_angle(s)
            if late is not None:
                interleave_scalar(late)
            if s < n_units - 1:
                scalar_classes(s)
            if s == n_units - 1:
                ot[s] = opool.tile([P, N], F32, name="o%d" % s, tag="o")
                last_half(s, 0)
                last_half(s, 1)
            copy_out(s + 3)
            quantise(s + 2)
            if late is not None:
                interleave_vector(late)
                store(late)
            if s == n_units - 2:
                relu_and_affine(s, nc.vector)
                interleave_scalar(s)
                interleave_vector(s)
                store(s)
